import numpy as np
import ml_dtypes


def mxq(x, axis, fmt="e4m3"):
    dtype, down = {"e4m3": (ml_dtypes.float8_e4m3fn, 7), "e5m2": (ml_dtypes.float8_e5m2, 14)}[fmt]
    v = np.moveaxis(np.asarray(x, np.float32).astype(ml_dtypes.bfloat16).astype(np.float64), axis, -1)
    blocks = v.reshape(v.shape[:-1] + (-1, 32))
    amax = np.abs(blocks).max(-1, keepdims=True)
    byte = np.maximum(np.where(amax > 0, np.frexp(amax)[1] - 1 + 127, 0) - down, 1)
    scale = np.exp2(byte - 127.0)
    codes = (blocks / scale).astype(np.float32).astype(dtype).astype(np.float64)
    return np.moveaxis((codes * scale).reshape(v.shape), -1, axis)


WIDE = False


def mx_kscale(k):
    if not WIDE:
        return np.ones(k)
    levels = np.array([10, -10, 5, -5, 0])
    a = np.random.permutation(np.resize(levels, k // 512 * 4)).reshape(k // 512, 4)
    idx = np.arange(k)
    return np.exp2(a[idx // 512, idx % 128 // 32])


BF16 = ml_dtypes.bfloat16


def bf(x):
    return np.asarray(x, np.float32).astype(BF16)


def f64(x):
    return np.asarray(x).astype(np.float64)


B, IN, OUT = 16384, 512, 512
EPS = 1e-5


def setup_inputs():
    s = mx_kscale(IN)
    return {"x": bf(np.random.standard_normal((B, IN)) * s),
            "weight": bf(np.random.standard_normal((OUT, IN)) / np.sqrt(IN) / s[None, :]),
            "bias": bf(np.random.standard_normal(OUT) * 0.1),
            "bn_weight": bf(1.0 + 0.1 * np.random.standard_normal(OUT)),
            "bn_bias": bf(np.random.standard_normal(OUT) * 0.1),
            "bn_mean": bf(np.random.standard_normal(OUT) * 0.1),
            "bn_var": bf(np.random.uniform(0.5, 1.5, OUT)),
            "gn_weight": bf(1.0 + 0.25 * np.sqrt(OUT) * np.random.standard_normal(OUT)),
            "gn_bias": bf(0.15 + 0.1 * np.random.standard_normal(OUT))}


def reference(x, weight, bias, bn_weight, bn_bias, bn_mean, bn_var, gn_weight, gn_bias):
    y = (mxq(f64(x), 1, "e4m3") @ mxq(f64(weight), 1, "e4m3").T) + f64(bias)
    y = (y - f64(bn_mean)) / np.sqrt(f64(bn_var) + EPS) * f64(bn_weight) + f64(bn_bias)
    y = y * 0.5 * (1.0 + np.tanh(0.797885 * y + 0.035677 * y * y * y))
    mean = np.mean(y, axis=1, keepdims=True)
    var = np.mean(y * y, axis=1, keepdims=True) - mean * mean
    gn = (y - mean) / np.sqrt(var + EPS) * f64(gn_weight) + f64(gn_bias)
    out = np.maximum(np.mean(gn, axis=1, keepdims=True), 0.0)
    return out

@@ -1,0 +1,333 @@
+import math
+from contextlib import ExitStack
+
+import concourse.mybir as mybir
+from concourse.masks import make_identity
+
+F32 = mybir.dt.float32
+BF16 = mybir.dt.bfloat16
+U32 = mybir.dt.uint32
+U8 = mybir.dt.uint8
+FP8X4 = mybir.dt.float8_e4m3fn_x4
+ACT = mybir.ActivationFunctionType
+ALU = mybir.AluOpType
+AX = mybir.AxisListType
+
+P = 128
+B, IN, OUT = 16384, 512, 512
+EPS = 1e-5
+C1, C2 = 0.797885, 0.035677
+NT = B // P
+GT = 4
+GW = GT * P
+NG = NT // GT
+CH = 8
+NJ = OUT // P
+
+FLOPS = 2 * B * IN * OUT
+
+
+def tile_modelnew_kernel(
+    tc, x, weight, bias, bn_weight, bn_bias, bn_mean, bn_var, gn_weight, gn_bias, out
+):
+    nc = tc.nc
+    with ExitStack() as ctx:
+        ctx.enter_context(tc.manual_schedule())
+        const = ctx.enter_context(tc.tile_pool(name="const", bufs=1))
+        xin = ctx.enter_context(tc.tile_pool(name="xin", bufs=NT // CH))
+        work2 = ctx.enter_context(tc.tile_pool(name="work2", bufs=2))
+        work3 = ctx.enter_context(tc.tile_pool(name="work3", bufs=3))
+        psum = ctx.enter_context(tc.psum_pool(name="psum", bufs=1))
+
+        w_sb = const.tile([P, NJ * IN], BF16)
+        nc.sync.dma_start(
+            out=w_sb[:].rearrange("p (j k) -> p j k", k=IN),
+            in_=weight.rearrange("(j p) k -> p j k", p=P),
+        )
+        pv = const.tile([P, P], BF16)
+        nc.vector.memset(pv[:], 0.0)
+        for v, vec in enumerate((bias, bn_weight, bn_bias, bn_mean, bn_var)):
+            nc.scalar.dma_start(
+                out=pv[NJ * v : NJ * v + NJ, :], in_=vec.rearrange("(j p) -> j p", p=P)
+            )
+        gwb = const.tile([P, OUT], BF16)
+        nc.scalar.dma_start(out=gwb[:], in_=gn_weight.partition_broadcast(P))
+        gbb = const.tile([P, OUT], BF16)
+        nc.scalar.dma_start(out=gbb[:], in_=gn_bias.partition_broadcast(P))
+
+        x_rows = x.rearrange("(p t) k -> p (t k)", t=NT)
+        x_sb = []
+        for c in range(NT // CH):
+            xc = xin.tile([P, CH * IN], BF16, tag="x")
+            nc.sync.dma_start(out=xc[:], in_=x_rows[:, c * CH * IN : (c + 1) * CH * IN])
+            x_sb.append(xc)
+
+        ident = const.tile([P, P], F32)
+        make_identity(nc, ident[:])
+        ident_b = const.tile([P, P], BF16)
+        make_identity(nc, ident_b[:])
+
+        def transposes(src, col0, b):
+            words = src[:].bitcast(F32)
+            xt = psum.tile([P, 2, 2, P], F32, tag="xt%d" % b, name="xt%d" % b)
+            for t2 in range(2):
+                for u in range(2):
+                    w0 = col0 // 2 + (2 * b + t2) * (IN // 2) + u * P
+                    nc.tensor.transpose(xt[:, t2, u, :], words[:, w0 : w0 + P], ident[:])
+            return xt
+
+        def copy_out(grouped, xt, b, engine):
+            gw32 = grouped[:].bitcast(F32)
+            dst = gw32[:, b * 512 : (b + 1) * 512].rearrange("p (t r u) -> p t r u", t=2, u=2)
+            srcv = xt[:].rearrange("p t u r -> p t r u")
+            if engine == "s":
+                nc.scalar.copy(out=dst, in_=srcv)
+            else:
+                nc.vector.tensor_copy(out=dst, in_=srcv)
+
+        wq = const.tile([P, OUT], U32, align_bytes=64)
+        ws = const.tile([P, OUT], U8, align_bytes=64)
+        w_grouped = work2.tile([P, GW * 4], BF16, tag="grouped", align_bytes=64)
+        copy_out(w_grouped, transposes(w_sb, 0, 0), 0, "s")
+        copy_out(w_grouped, transposes(w_sb, 0, 1), 1, "v")
+
+        pT = psum.tile([P, P], BF16, tag="yT0", name="pT")
+        nc.tensor.transpose(pT[:], pv[:], ident_b[:])
+        pf = const.tile([P, 5 * NJ], F32)
+        nc.vector.tensor_copy(out=pf[:], in_=pT[:, 0 : 5 * NJ])
+        nc.vector.quantize_mx(out=wq[:].bitcast(FP8X4), scales=ws[:], in_=w_grouped[:])
+        eps1 = const.tile([P, 1], F32)
+        nc.vector.memset(eps1[:], EPS)
+        eps2 = const.tile([P, 1], F32)
+        nc.vector.memset(eps2[:], EPS * OUT * OUT)
+        a_c = const.tile([P, NJ], F32)
+        b_c = const.tile([P, NJ], F32)
+        nc.scalar.activation(
+            out=a_c[:], in_=pf[:, 4 * NJ : 5 * NJ], func=ACT.Sqrt, bias=eps1[:, 0:1], scale=1.0
+        )
+        nc.vector.reciprocal(out=a_c[:], in_=a_c[:])
+        nc.vector.tensor_tensor(out=a_c[:], in0=a_c[:], in1=pf[:, NJ : 2 * NJ], op=ALU.mult)
+        nc.vector.tensor_tensor(
+            out=b_c[:], in0=pf[:, 0:NJ], in1=pf[:, 3 * NJ : 4 * NJ], op=ALU.subtract
+        )
+        nc.vector.tensor_tensor(out=b_c[:], in0=b_c[:], in1=a_c[:], op=ALU.mult)
+        nc.vector.tensor_tensor(out=b_c[:], in0=b_c[:], in1=pf[:, 2 * NJ : 3 * NJ], op=ALU.add)
+        r = math.sqrt(C2)
+        sc1 = const.tile([P, NJ], F32)
+        bi1 = const.tile([P, NJ], F32)
+        s_c = const.tile([P, NJ], F32)
+        sc2 = const.tile([P, NJ], F32)
+        bi2 = const.tile([P, NJ], F32)
+        bb = const.tile([P, NJ], F32)
+        nc.vector.tensor_scalar(out=sc1[:], in0=a_c[:], scalar1=r, scalar2=None, op0=ALU.mult)
+        nc.vector.tensor_scalar(out=bi1[:], in0=b_c[:], scalar1=1.5 * r, scalar2=None, op0=ALU.mult)
+        nc.vector.tensor_tensor(out=bb[:], in0=b_c[:], in1=b_c[:], op=ALU.mult)
+        nc.vector.tensor_scalar(
+            out=s_c[:], in0=bb[:], scalar1=0.75 * C2, scalar2=C1, op0=ALU.mult, op1=ALU.add
+        )
+        nc.vector.tensor_scalar(out=sc2[:], in0=a_c[:], scalar1=2.0, scalar2=None, op0=ALU.mult)
+        nc.vector.tensor_scalar(
+            out=bb[:], in0=bb[:], scalar1=2.0 * C2, scalar2=2.0 * C1, op0=ALU.mult, op1=ALU.add
+        )
+        nc.vector.tensor_tensor(out=bi2[:], in0=bb[:], in1=b_c[:], op=ALU.mult)
+
+        nh_sgw = const.tile([P, 1], F32)
+        nc.vector.tensor_reduce(out=nh_sgw[:], in_=gwb[:], axis=AX.X, op=ALU.add)
+        nc.vector.tensor_scalar(
+            out=nh_sgw[:], in0=nh_sgw[:], scalar1=-0.5, scalar2=None, op0=ALU.mult
+        )
+        mgb = const.tile([P, 1], F32)
+        nc.vector.tensor_reduce(out=mgb[:], in_=gbb[:], axis=AX.X, op=ALU.add)
+        nc.vector.tensor_scalar(
+            out=mgb[:], in0=mgb[:], scalar1=1.0 / OUT, scalar2=None, op0=ALU.mult
+        )
+
+        st = const.tile([P, NT, 6], F32)
+        traw = const.tile([P, NT], F32)
+        junk = const.tile([P, OUT], F32)
+
+        banks_of = {}
+        grouped_of = {}
+        xq_of = {}
+        acc_of = {}
+        c_of = {}
+        z_of = {}
+        yT_of = {}
+
+        def ok(g):
+            return 0 <= g < NG
+
+        def pe_xt(g, b):
+            if ok(g):
+                banks_of[(g, b)] = transposes(x_sb[(g * GT) // CH], ((g * GT) % CH) * IN, b)
+
+        def evac(g, b, engine):
+            if ok(g):
+                if b == 0:
+                    grouped_of[g] = work2.tile(
+                        [P, GW * 4], BF16, tag="grouped", name="grouped", align_bytes=64
+                    )
+                copy_out(grouped_of[g], banks_of[(g, b)], b, engine)
+
+        def quant(g):
+            if ok(g):
+                xq = work2.tile([P, GW], U32, tag="xq", align_bytes=64)
+                xs = work2.tile([P, GW], U8, tag="xs", align_bytes=64)
+                nc.vector.quantize_mx(out=xq[:].bitcast(FP8X4), scales=xs[:], in_=grouped_of[g][:])
+                xq_of[g] = (xq, xs)
+
+        def mx(g, js):
+            if ok(g):
+                xq, xs = xq_of[g]
+                for j in js:
+                    acc = psum.tile([P, GW], F32, tag="acc%d" % j, name="acc%d" % j)
+                    nc.tensor.matmul_mx(
+                        out=acc[:],
+                        lhsT=wq[:, j * P : (j + 1) * P].bitcast(FP8X4),
+                        lhsT_scale=ws[:, j * P : (j + 1) * P],
+                        rhs=xq[:].bitcast(FP8X4),
+                        rhs_scale=xs[:],
+                        start=True,
+                        stop=True,
+                    )
+                    acc_of[(g, j)] = acc
+
+        def s_square_z(g, js):
+            if ok(g):
+                if js[0] == 0:
+                    c_of[g] = work3.tile([P, NJ * GW], F32, tag="c", name="c")
+                    z_of[g] = work3.tile([P, NJ * GW], F32, tag="z", name="z")
+                for j in js:
+                    nc.scalar.activation(
+                        out=z_of[g][:, j * GW : (j + 1) * GW],
+                        in_=acc_of[(g, j)][:],
+                        func=ACT.Identity,
+                        bias=b_c[:, j : j + 1],
+                        scale=a_c[:, j : j + 1],
+                    )
+                    nc.scalar.activation(
+                        out=c_of[g][:, j * GW : (j + 1) * GW],
+                        in_=acc_of[(g, j)][:],
+                        func=ACT.Square,
+                        bias=bi1[:, j : j + 1],
+                        scale=sc1[:, j : j + 1],
+                    )
+
+        def v_cubic(g, js):
+            if ok(g):
+                for j in js:
+                    cj = c_of[g][:, j * GW : (j + 1) * GW]
+                    nc.vector.scalar_tensor_tensor(
+                        out=cj,
+                        in0=cj,
+                        scalar=s_c[:, j : j + 1],
+                        in1=acc_of[(g, j)][:],
+                        op0=ALU.add,
+                        op1=ALU.mult,
+                    )
+
+        def s_sigmoid(g, js):
+            if ok(g):
+                for j in js:
+                    cj = c_of[g][:, j * GW : (j + 1) * GW]
+                    nc.scalar.activation(
+                        out=cj,
+                        in_=cj,
+                        func=ACT.Sigmoid,
+                        bias=bi2[:, j : j + 1],
+                        scale=sc2[:, j : j + 1],
+                    )
+
+        def g_mul(g, js):
+            if ok(g):
+                for j in js:
+                    cj = c_of[g][:, j * GW : (j + 1) * GW]
+                    nc.gpsimd.tensor_tensor(
+                        out=cj, in0=cj, in1=z_of[g][:, j * GW : (j + 1) * GW], op=ALU.mult
+                    )
+
+        def pe_yt(g, t):
+            if ok(g):
+                yT = psum.tile([P, OUT], F32, tag="yT%d" % (t % 2), name="yT%d" % (t % 2))
+                for j in range(NJ):
+                    nc.tensor.transpose(
+                        yT[:, j * P : (j + 1) * P],
+                        c_of[g][:, j * GW + t * P : j * GW + (t + 1) * P],
+                        ident[:],
+                    )
+                yT_of[(g, t)] = yT
+
+        def v_bn(g, t):
+            if ok(g):
+                nc.vector.bn_stats(out=st[:, g * GT + t, :], in_=yT_of[(g, t)][:])
+
+        def v_dot(g, t):
+            if ok(g):
+                yT = yT_of[(g, t)]
+                tt = g * GT + t
+                nc.vector.scalar_tensor_tensor(
+                    out=junk[:],
+                    in0=yT[:],
+                    scalar=1.0,
+                    in1=gwb[:],
+                    op0=ALU.mult,
+                    op1=ALU.mult,
+                    accum_out=traw[:, tt : tt + 1],
+                )
+
+        for g in range(-2, NG + 1):
+            e1 = "v" if g % 2 == 0 else "s"
+            pe_xt(g + 2, 0)
+            s_square_z(g, (0, 1))
+            v_cubic(g, (0,))
+            quant(g + 1)
+            v_cubic(g, (1,))
+            evac(g + 2, 0, "s")
+            pe_yt(g - 1, 0)
+            pe_yt(g - 1, 1)
+            mx(g + 1, (0, 1))
+            s_sigmoid(g, (0, 1))
+            g_mul(g, (0, 1))
+            v_bn(g - 1, 0)
+            v_dot(g - 1, 0)
+            v_bn(g - 1, 1)
+            v_dot(g - 1, 1)
+            pe_yt(g - 1, 2)
+            pe_xt(g + 2, 1)
+            s_square_z(g, (2, 3))
+            v_cubic(g, (2,))
+            v_bn(g - 1, 2)
+            v_cubic(g, (3,))
+            v_dot(g - 1, 2)
+            pe_yt(g - 1, 3)
+            mx(g + 1, (2, 3))
+            if e1 == "s":
+                evac(g + 2, 1, "s")
+            s_sigmoid(g, (2, 3))
+            g_mul(g, (2, 3))
+            v_bn(g - 1, 3)
+            v_dot(g - 1, 3)
+            if e1 == "v":
+                evac(g + 2, 1, "v")
+
+        s = const.tile([P, NT], F32)
+        d = const.tile([P, NT], F32)
+        vs = const.tile([P, NT], F32)
+        nc.vector.tensor_tensor(out=s[:], in0=st[:, :, 1], in1=st[:, :, 4], op=ALU.add)
+        nc.vector.tensor_tensor(out=d[:], in0=st[:, :, 1], in1=st[:, :, 4], op=ALU.subtract)
+        nc.vector.tensor_tensor(out=vs[:], in0=st[:, :, 2], in1=st[:, :, 5], op=ALU.add)
+        nc.vector.tensor_tensor(out=d[:], in0=d[:], in1=d[:], op=ALU.mult)
+        nc.vector.scalar_tensor_tensor(
+            out=vs[:], in0=d[:], scalar=float(OUT // 4), in1=vs[:], op0=ALU.mult, op1=ALU.add
+        )
+        nc.scalar.activation(
+            out=vs[:], in_=vs[:], func=ACT.Sqrt, bias=eps2[:, 0:1], scale=float(OUT)
+        )
+        nc.vector.reciprocal(out=vs[:], in_=vs[:])
+        nc.vector.scalar_tensor_tensor(
+            out=s[:], in0=s[:], scalar=nh_sgw[:, 0:1], in1=traw[:], op0=ALU.mult, op1=ALU.add
+        )
+        nc.vector.tensor_tensor(out=s[:], in0=s[:], in1=vs[:], op=ALU.mult)
+        res = const.tile([P, NT], F32)
+        nc.scalar.activation(out=res[:], in_=s[:], func=ACT.Relu, bias=mgb[:, 0:1], scale=1.0)
+        nc.sync.dma_start(out=out.rearrange("(p t) o -> p (t o)", t=NT), in_=res[:])

@@ -21,7 +21,7 @@ NT = B // P
 GT = 4
 GW = GT * P
 NG = NT // GT
-CH = 8
+CHUNKS = (4, 4) + (8,) * 15
 NJ = OUT // P
 
 FLOPS = 2 * B * IN * OUT
@@ -34,7 +34,7 @@ def tile_modelnew_kernel(
     with ExitStack() as ctx:
         ctx.enter_context(tc.manual_schedule())
         const = ctx.enter_context(tc.tile_pool(name="const", bufs=1))
-        xin = ctx.enter_context(tc.tile_pool(name="xin", bufs=NT // CH))
+        xin = ctx.enter_context(tc.tile_pool(name="xin", bufs=1))
         work2 = ctx.enter_context(tc.tile_pool(name="work2", bufs=2))
         work3 = ctx.enter_context(tc.tile_pool(name="work3", bufs=3))
         psum = ctx.enter_context(tc.psum_pool(name="psum", bufs=1))
@@ -51,16 +51,20 @@ def tile_modelnew_kernel(
                 out=pv[NJ * v : NJ * v + NJ, :], in_=vec.rearrange("(j p) -> j p", p=P)
             )
         gwb = const.tile([P, OUT], BF16)
-        nc.scalar.dma_start(out=gwb[:], in_=gn_weight.partition_broadcast(P))
         gbb = const.tile([P, OUT], BF16)
-        nc.scalar.dma_start(out=gbb[:], in_=gn_bias.partition_broadcast(P))
 
         x_rows = x.rearrange("(p t) k -> p (t k)", t=NT)
-        x_sb = []
-        for c in range(NT // CH):
-            xc = xin.tile([P, CH * IN], BF16, tag="x")
-            nc.sync.dma_start(out=xc[:], in_=x_rows[:, c * CH * IN : (c + 1) * CH * IN])
-            x_sb.append(xc)
+        x_of = []
+        t0 = 0
+        for c, n_tiles in enumerate(CHUNKS):
+            xc = xin.tile([P, n_tiles * IN], BF16, tag="x%d" % c, name="xc")
+            nc.sync.dma_start(out=xc[:], in_=x_rows[:, t0 * IN : (t0 + n_tiles) * IN])
+            for q in range(n_tiles // GT):
+                x_of.append((xc, q * GT * IN))
+            t0 += n_tiles
+            if c == 2:
+                nc.sync.dma_start(out=gwb[:], in_=gn_weight.partition_broadcast(P))
+                nc.sync.dma_start(out=gbb[:], in_=gn_bias.partition_broadcast(P))
 
         ident = const.tile([P, P], F32)
         make_identity(nc, ident[:])
@@ -132,15 +136,17 @@ def tile_modelnew_kernel(
         nc.vector.tensor_tensor(out=bi2[:], in0=bb[:], in1=b_c[:], op=ALU.mult)
 
         nh_sgw = const.tile([P, 1], F32)
-        nc.vector.tensor_reduce(out=nh_sgw[:], in_=gwb[:], axis=AX.X, op=ALU.add)
-        nc.vector.tensor_scalar(
-            out=nh_sgw[:], in0=nh_sgw[:], scalar1=-0.5, scalar2=None, op0=ALU.mult
-        )
         mgb = const.tile([P, 1], F32)
-        nc.vector.tensor_reduce(out=mgb[:], in_=gbb[:], axis=AX.X, op=ALU.add)
-        nc.vector.tensor_scalar(
-            out=mgb[:], in0=mgb[:], scalar1=1.0 / OUT, scalar2=None, op0=ALU.mult
-        )
+
+        def row_constants():
+            nc.vector.tensor_reduce(out=nh_sgw[:], in_=gwb[:], axis=AX.X, op=ALU.add)
+            nc.vector.tensor_scalar(
+                out=nh_sgw[:], in0=nh_sgw[:], scalar1=-0.5, scalar2=None, op0=ALU.mult
+            )
+            nc.vector.tensor_reduce(out=mgb[:], in_=gbb[:], axis=AX.X, op=ALU.add)
+            nc.vector.tensor_scalar(
+                out=mgb[:], in0=mgb[:], scalar1=1.0 / OUT, scalar2=None, op0=ALU.mult
+            )
 
         st = const.tile([P, NT, 6], F32)
         traw = const.tile([P, NT], F32)
@@ -159,7 +165,7 @@ def tile_modelnew_kernel(
 
         def pe_xt(g, b):
             if ok(g):
-                banks_of[(g, b)] = transposes(x_sb[(g * GT) // CH], ((g * GT) % CH) * IN, b)
+                banks_of[(g, b)] = transposes(x_of[g][0], x_of[g][1], b)
 
         def evac(g, b, engine):
             if ok(g):
@@ -275,40 +281,43 @@ def tile_modelnew_kernel(
                     accum_out=traw[:, tt : tt + 1],
                 )
 
-        for g in range(-2, NG + 1):
+        for g in range(-2, NG + 2):
             e1 = "v" if g % 2 == 0 else "s"
             pe_xt(g + 2, 0)
             s_square_z(g, (0, 1))
-            v_cubic(g, (0,))
-            quant(g + 1)
-            v_cubic(g, (1,))
+            v_bn(g - 2, 0)
+            v_dot(g - 2, 0)
+            v_bn(g - 2, 1)
+            v_dot(g - 2, 1)
             evac(g + 2, 0, "s")
-            pe_yt(g - 1, 0)
-            pe_yt(g - 1, 1)
+            pe_yt(g - 2, 2)
+            pe_yt(g - 2, 3)
+            quant(g + 1)
+            s_sigmoid(g - 1, (2, 3))
+            g_mul(g - 1, (2, 3))
+            v_cubic(g, (0, 1))
             mx(g + 1, (0, 1))
-            s_sigmoid(g, (0, 1))
-            g_mul(g, (0, 1))
-            v_bn(g - 1, 0)
-            v_dot(g - 1, 0)
-            v_bn(g - 1, 1)
-            v_dot(g - 1, 1)
-            pe_yt(g - 1, 2)
             pe_xt(g + 2, 1)
             s_square_z(g, (2, 3))
-            v_cubic(g, (2,))
-            v_bn(g - 1, 2)
-            v_cubic(g, (3,))
-            v_dot(g - 1, 2)
-            pe_yt(g - 1, 3)
-            mx(g + 1, (2, 3))
+            v_bn(g - 2, 2)
+            v_dot(g - 2, 2)
+            v_bn(g - 2, 3)
+            v_dot(g - 2, 3)
+            pe_yt(g - 1, 0)
+            pe_yt(g - 1, 1)
             if e1 == "s":
                 evac(g + 2, 1, "s")
-            s_sigmoid(g, (2, 3))
-            g_mul(g, (2, 3))
-            v_bn(g - 1, 3)
-            v_dot(g - 1, 3)
+            v_cubic(g, (2, 3))
+            mx(g + 1, (2, 3))
+            s_sigmoid(g, (0, 1))
+            g_mul(g, (0, 1))
             if e1 == "v":
                 evac(g + 2, 1, "v")
+            if g == 1:
+                row_constants()
+
+        warm = const.tile([P, 1], F32)
+        nc.scalar.activation(out=warm[:], in_=eps1[:], func=ACT.Sqrt, bias=eps1[:, 0:1], scale=1.0)
 
         s = const.tile([P, NT], F32)
         d = const.tile([P, NT], F32)

@@ -23,6 +23,7 @@ GW = GT * P
 NG = NT // GT
 CHUNKS = (4, 4) + (8,) * 15
 NJ = OUT // P
+N_PE = 4
 
 FLOPS = 2 * B * IN * OUT
 
@@ -46,7 +47,7 @@ def tile_modelnew_kernel(
         )
         pv = const.tile([P, P], BF16)
         nc.vector.memset(pv[:], 0.0)
-        for v, vec in enumerate((bias, bn_weight, bn_bias, bn_mean, bn_var)):
+        for v, vec in enumerate((bias, bn_weight, bn_bias, bn_mean, bn_var, gn_weight)):
             nc.scalar.dma_start(
                 out=pv[NJ * v : NJ * v + NJ, :], in_=vec.rearrange("(j p) -> j p", p=P)
             )
@@ -73,7 +74,7 @@ def tile_modelnew_kernel(
 
         def transposes(src, col0, b):
             words = src[:].bitcast(F32)
-            xt = psum.tile([P, 2, 2, P], F32, tag="xt%d" % b, name="xt%d" % b)
+            xt = psum.tile([P, 2, 2, P], F32, tag="xt", name="xt")
             for t2 in range(2):
                 for u in range(2):
                     w0 = col0 // 2 + (2 * b + t2) * (IN // 2) + u * P
@@ -97,8 +98,8 @@ def tile_modelnew_kernel(
 
         pT = psum.tile([P, P], BF16, tag="yT0", name="pT")
         nc.tensor.transpose(pT[:], pv[:], ident_b[:])
-        pf = const.tile([P, 5 * NJ], F32)
-        nc.vector.tensor_copy(out=pf[:], in_=pT[:, 0 : 5 * NJ])
+        pf = const.tile([P, 6 * NJ], F32)
+        nc.vector.tensor_copy(out=pf[:], in_=pT[:, 0 : 6 * NJ])
         nc.vector.quantize_mx(out=wq[:].bitcast(FP8X4), scales=ws[:], in_=w_grouped[:])
         eps1 = const.tile([P, 1], F32)
         nc.vector.memset(eps1[:], EPS)
@@ -135,6 +136,11 @@ def tile_modelnew_kernel(
         )
         nc.vector.tensor_tensor(out=bi2[:], in0=bb[:], in1=b_c[:], op=ALU.mult)
 
+        gm = const.tile([P, NJ, 2], F32)
+        nc.vector.memset(gm[:], 1.0)
+        nc.vector.tensor_copy(out=gm[:, :, 0], in_=pf[:, 5 * NJ : 6 * NJ])
+        ts = psum.tile([P, NT, 2], F32, tag="ts", name="ts")
+
         nh_sgw = const.tile([P, 1], F32)
         mgb = const.tile([P, 1], F32)
 
@@ -150,7 +156,7 @@ def tile_modelnew_kernel(
 
         st = const.tile([P, NT, 6], F32)
         traw = const.tile([P, NT], F32)
-        junk = const.tile([P, OUT], F32)
+        junk = const.tile([P, OUT], F32) if N_PE < GT else None
 
         banks_of = {}
         grouped_of = {}
@@ -263,12 +269,23 @@ def tile_modelnew_kernel(
                     )
                 yT_of[(g, t)] = yT
 
+        def pe_dot(g, t):
+            if ok(g) and t < N_PE:
+                for j in range(NJ):
+                    nc.tensor.matmul(
+                        out=ts[:, g * GT + t, :],
+                        lhsT=c_of[g][:, j * GW + t * P : j * GW + (t + 1) * P],
+                        rhs=gm[:, j, :],
+                        start=(j == 0),
+                        stop=(j == NJ - 1),
+                    )
+
         def v_bn(g, t):
             if ok(g):
                 nc.vector.bn_stats(out=st[:, g * GT + t, :], in_=yT_of[(g, t)][:])
 
         def v_dot(g, t):
-            if ok(g):
+            if ok(g) and t >= N_PE:
                 yT = yT_of[(g, t)]
                 tt = g * GT + t
                 nc.vector.scalar_tensor_tensor(
@@ -282,16 +299,17 @@ def tile_modelnew_kernel(
                 )
 
         for g in range(-2, NG + 2):
-            e1 = "v" if g % 2 == 0 else "s"
             pe_xt(g + 2, 0)
             s_square_z(g, (0, 1))
             v_bn(g - 2, 0)
             v_dot(g - 2, 0)
             v_bn(g - 2, 1)
             v_dot(g - 2, 1)
-            evac(g + 2, 0, "s")
+            evac(g + 2, 0, "v")
             pe_yt(g - 2, 2)
+            pe_dot(g - 2, 2)
             pe_yt(g - 2, 3)
+            pe_dot(g - 2, 3)
             quant(g + 1)
             s_sigmoid(g - 1, (2, 3))
             g_mul(g - 1, (2, 3))
@@ -303,22 +321,26 @@ def tile_modelnew_kernel(
             v_dot(g - 2, 2)
             v_bn(g - 2, 3)
             v_dot(g - 2, 3)
+            evac(g + 2, 1, "v")
             pe_yt(g - 1, 0)
+            pe_dot(g - 1, 0)
             pe_yt(g - 1, 1)
-            if e1 == "s":
-                evac(g + 2, 1, "s")
+            pe_dot(g - 1, 1)
             v_cubic(g, (2, 3))
             mx(g + 1, (2, 3))
             s_sigmoid(g, (0, 1))
             g_mul(g, (0, 1))
-            if e1 == "v":
-                evac(g + 2, 1, "v")
             if g == 1:
                 row_constants()
 
         warm = const.tile([P, 1], F32)
         nc.scalar.activation(out=warm[:], in_=eps1[:], func=ACT.Sqrt, bias=eps1[:, 0:1], scale=1.0)
 
+        if N_PE > 0:
+            nc.vector.tensor_copy(
+                out=traw[:].rearrange("p (g t) -> p g t", t=GT)[:, :, 0:N_PE],
+                in_=ts[:].rearrange("p (g t) c -> p g t c", t=GT)[:, :, 0:N_PE, 0],
+            )
         s = const.tile([P, NT], F32)
         d = const.tile([P, NT], F32)
         vs = const.tile([P, NT], F32)

@@ -23,7 +23,7 @@ GW = GT * P
 NG = NT // GT
 CHUNKS = (4, 4) + (8,) * 15
 NJ = OUT // P
-N_PE = 4
+V_COPIES = (-2, -1, 0, 1, 7, 13, 19, 25)
 
 FLOPS = 2 * B * IN * OUT
 
@@ -47,7 +47,7 @@ def tile_modelnew_kernel(
         )
         pv = const.tile([P, P], BF16)
         nc.vector.memset(pv[:], 0.0)
-        for v, vec in enumerate((bias, bn_weight, bn_bias, bn_mean, bn_var, gn_weight)):
+        for v, vec in enumerate((bias, bn_weight, bn_bias, bn_mean, bn_var)):
             nc.scalar.dma_start(
                 out=pv[NJ * v : NJ * v + NJ, :], in_=vec.rearrange("(j p) -> j p", p=P)
             )
@@ -74,7 +74,7 @@ def tile_modelnew_kernel(
 
         def transposes(src, col0, b):
             words = src[:].bitcast(F32)
-            xt = psum.tile([P, 2, 2, P], F32, tag="xt", name="xt")
+            xt = psum.tile([P, 2, 2, P], F32, tag="xt%d" % b, name="xt%d" % b)
             for t2 in range(2):
                 for u in range(2):
                     w0 = col0 // 2 + (2 * b + t2) * (IN // 2) + u * P
@@ -98,8 +98,8 @@ def tile_modelnew_kernel(
 
         pT = psum.tile([P, P], BF16, tag="yT0", name="pT")
         nc.tensor.transpose(pT[:], pv[:], ident_b[:])
-        pf = const.tile([P, 6 * NJ], F32)
-        nc.vector.tensor_copy(out=pf[:], in_=pT[:, 0 : 6 * NJ])
+        pf = const.tile([P, 5 * NJ], F32)
+        nc.vector.tensor_copy(out=pf[:], in_=pT[:, 0 : 5 * NJ])
         nc.vector.quantize_mx(out=wq[:].bitcast(FP8X4), scales=ws[:], in_=w_grouped[:])
         eps1 = const.tile([P, 1], F32)
         nc.vector.memset(eps1[:], EPS)
@@ -136,11 +136,6 @@ def tile_modelnew_kernel(
         )
         nc.vector.tensor_tensor(out=bi2[:], in0=bb[:], in1=b_c[:], op=ALU.mult)
 
-        gm = const.tile([P, NJ, 2], F32)
-        nc.vector.memset(gm[:], 1.0)
-        nc.vector.tensor_copy(out=gm[:, :, 0], in_=pf[:, 5 * NJ : 6 * NJ])
-        ts = psum.tile([P, NT, 2], F32, tag="ts", name="ts")
-
         nh_sgw = const.tile([P, 1], F32)
         mgb = const.tile([P, 1], F32)
 
@@ -156,7 +151,7 @@ def tile_modelnew_kernel(
 
         st = const.tile([P, NT, 6], F32)
         traw = const.tile([P, NT], F32)
-        junk = const.tile([P, OUT], F32) if N_PE < GT else None
+        junk = const.tile([P, OUT], F32)
 
         banks_of = {}
         grouped_of = {}
@@ -204,19 +199,23 @@ def tile_modelnew_kernel(
                     )
                     acc_of[(g, j)] = acc
 
+        def z_on_vector(g, j):
+            return (g == 0 and j == 1) or (g == 1 and j in (1, 3))
+
         def s_square_z(g, js):
             if ok(g):
                 if js[0] == 0:
                     c_of[g] = work3.tile([P, NJ * GW], F32, tag="c", name="c")
                     z_of[g] = work3.tile([P, NJ * GW], F32, tag="z", name="z")
                 for j in js:
-                    nc.scalar.activation(
-                        out=z_of[g][:, j * GW : (j + 1) * GW],
-                        in_=acc_of[(g, j)][:],
-                        func=ACT.Identity,
-                        bias=b_c[:, j : j + 1],
-                        scale=a_c[:, j : j + 1],
-                    )
+                    if not z_on_vector(g, j):
+                        nc.scalar.activation(
+                            out=z_of[g][:, j * GW : (j + 1) * GW],
+                            in_=acc_of[(g, j)][:],
+                            func=ACT.Identity,
+                            bias=b_c[:, j : j + 1],
+                            scale=a_c[:, j : j + 1],
+                        )
                     nc.scalar.activation(
                         out=c_of[g][:, j * GW : (j + 1) * GW],
                         in_=acc_of[(g, j)][:],
@@ -237,6 +236,15 @@ def tile_modelnew_kernel(
                         op0=ALU.add,
                         op1=ALU.mult,
                     )
+                    if z_on_vector(g, j):
+                        nc.vector.tensor_scalar(
+                            out=z_of[g][:, j * GW : (j + 1) * GW],
+                            in0=acc_of[(g, j)][:],
+                            scalar1=a_c[:, j : j + 1],
+                            scalar2=b_c[:, j : j + 1],
+                            op0=ALU.mult,
+                            op1=ALU.add,
+                        )
 
         def s_sigmoid(g, js):
             if ok(g):
@@ -269,23 +277,12 @@ def tile_modelnew_kernel(
                     )
                 yT_of[(g, t)] = yT
 
-        def pe_dot(g, t):
-            if ok(g) and t < N_PE:
-                for j in range(NJ):
-                    nc.tensor.matmul(
-                        out=ts[:, g * GT + t, :],
-                        lhsT=c_of[g][:, j * GW + t * P : j * GW + (t + 1) * P],
-                        rhs=gm[:, j, :],
-                        start=(j == 0),
-                        stop=(j == NJ - 1),
-                    )
-
         def v_bn(g, t):
             if ok(g):
                 nc.vector.bn_stats(out=st[:, g * GT + t, :], in_=yT_of[(g, t)][:])
 
         def v_dot(g, t):
-            if ok(g) and t >= N_PE:
+            if ok(g):
                 yT = yT_of[(g, t)]
                 tt = g * GT + t
                 nc.vector.scalar_tensor_tensor(
@@ -299,17 +296,17 @@ def tile_modelnew_kernel(
                 )
 
         for g in range(-2, NG + 2):
+            e0 = "v" if g in (0, 1) else "s"
+            e1 = "v" if g in V_COPIES else "s"
             pe_xt(g + 2, 0)
             s_square_z(g, (0, 1))
             v_bn(g - 2, 0)
             v_dot(g - 2, 0)
             v_bn(g - 2, 1)
             v_dot(g - 2, 1)
-            evac(g + 2, 0, "v")
+            evac(g + 2, 0, e0)
             pe_yt(g - 2, 2)
-            pe_dot(g - 2, 2)
             pe_yt(g - 2, 3)
-            pe_dot(g - 2, 3)
             quant(g + 1)
             s_sigmoid(g - 1, (2, 3))
             g_mul(g - 1, (2, 3))
@@ -321,26 +318,22 @@ def tile_modelnew_kernel(
             v_dot(g - 2, 2)
             v_bn(g - 2, 3)
             v_dot(g - 2, 3)
-            evac(g + 2, 1, "v")
             pe_yt(g - 1, 0)
-            pe_dot(g - 1, 0)
             pe_yt(g - 1, 1)
-            pe_dot(g - 1, 1)
+            if e1 == "s":
+                evac(g + 2, 1, "s")
             v_cubic(g, (2, 3))
             mx(g + 1, (2, 3))
             s_sigmoid(g, (0, 1))
             g_mul(g, (0, 1))
+            if e1 == "v":
+                evac(g + 2, 1, "v")
             if g == 1:
                 row_constants()
 
         warm = const.tile([P, 1], F32)
         nc.scalar.activation(out=warm[:], in_=eps1[:], func=ACT.Sqrt, bias=eps1[:, 0:1], scale=1.0)
 
-        if N_PE > 0:
-            nc.vector.tensor_copy(
-                out=traw[:].rearrange("p (g t) -> p g t", t=GT)[:, :, 0:N_PE],
-                in_=ts[:].rearrange("p (g t) c -> p g t c", t=GT)[:, :, 0:N_PE, 0],
-            )
         s = const.tile([P, NT], F32)
         d = const.tile([P, NT], F32)
         vs = const.tile([P, NT], F32)

@@ -23,7 +23,7 @@ GW = GT * P
 NG = NT // GT
 CHUNKS = (4, 4) + (8,) * 15
 NJ = OUT // P
-V_COPIES = (-2, -1, 0, 1, 7, 13, 19, 25)
+V_COPIES = (7, 13, 19, 25)
 
 FLOPS = 2 * B * IN * OUT
 
@@ -46,11 +46,21 @@ def tile_modelnew_kernel(
             in_=weight.rearrange("(j p) k -> p j k", p=P),
         )
         pv = const.tile([P, P], BF16)
-        nc.vector.memset(pv[:], 0.0)
+        nc.gpsimd.memset(pv[:], 0.0)
         for v, vec in enumerate((bias, bn_weight, bn_bias, bn_mean, bn_var)):
             nc.scalar.dma_start(
                 out=pv[NJ * v : NJ * v + NJ, :], in_=vec.rearrange("(j p) -> j p", p=P)
             )
+        zero = const.tile([P, 1], F32)
+        nc.vector.memset(zero[:], 0.0)
+        mhalf = const.tile([P, NJ], F32)
+        nc.vector.memset(mhalf[:], -0.5)
+        eps1 = const.tile([P, 1], F32)
+        nc.vector.memset(eps1[:], EPS)
+        eps2 = const.tile([P, 1], F32)
+        nc.vector.memset(eps2[:], EPS * OUT * OUT)
+        warm0 = const.tile([P, 1], F32)
+        nc.scalar.activation(out=warm0[:], in_=zero[:], func=ACT.Sigmoid, bias=zero[:, 0:1], scale=1.0)
         gwb = const.tile([P, OUT], BF16)
         gbb = const.tile([P, OUT], BF16)
 
@@ -72,9 +82,9 @@ def tile_modelnew_kernel(
         ident_b = const.tile([P, P], BF16)
         make_identity(nc, ident_b[:])
 
-        def transposes(src, col0, b):
+        def transposes(src, col0, b, tag):
             words = src[:].bitcast(F32)
-            xt = psum.tile([P, 2, 2, P], F32, tag="xt%d" % b, name="xt%d" % b)
+            xt = psum.tile([P, 2, 2, P], F32, tag=tag, name="xt_" + tag)
             for t2 in range(2):
                 for u in range(2):
                     w0 = col0 // 2 + (2 * b + t2) * (IN // 2) + u * P
@@ -92,31 +102,9 @@ def tile_modelnew_kernel(
 
         wq = const.tile([P, OUT], U32, align_bytes=64)
         ws = const.tile([P, OUT], U8, align_bytes=64)
-        w_grouped = work2.tile([P, GW * 4], BF16, tag="grouped", align_bytes=64)
-        copy_out(w_grouped, transposes(w_sb, 0, 0), 0, "s")
-        copy_out(w_grouped, transposes(w_sb, 0, 1), 1, "v")
-
-        pT = psum.tile([P, P], BF16, tag="yT0", name="pT")
-        nc.tensor.transpose(pT[:], pv[:], ident_b[:])
         pf = const.tile([P, 5 * NJ], F32)
-        nc.vector.tensor_copy(out=pf[:], in_=pT[:, 0 : 5 * NJ])
-        nc.vector.quantize_mx(out=wq[:].bitcast(FP8X4), scales=ws[:], in_=w_grouped[:])
-        eps1 = const.tile([P, 1], F32)
-        nc.vector.memset(eps1[:], EPS)
-        eps2 = const.tile([P, 1], F32)
-        nc.vector.memset(eps2[:], EPS * OUT * OUT)
         a_c = const.tile([P, NJ], F32)
         b_c = const.tile([P, NJ], F32)
-        nc.scalar.activation(
-            out=a_c[:], in_=pf[:, 4 * NJ : 5 * NJ], func=ACT.Sqrt, bias=eps1[:, 0:1], scale=1.0
-        )
-        nc.vector.reciprocal(out=a_c[:], in_=a_c[:])
-        nc.vector.tensor_tensor(out=a_c[:], in0=a_c[:], in1=pf[:, NJ : 2 * NJ], op=ALU.mult)
-        nc.vector.tensor_tensor(
-            out=b_c[:], in0=pf[:, 0:NJ], in1=pf[:, 3 * NJ : 4 * NJ], op=ALU.subtract
-        )
-        nc.vector.tensor_tensor(out=b_c[:], in0=b_c[:], in1=a_c[:], op=ALU.mult)
-        nc.vector.tensor_tensor(out=b_c[:], in0=b_c[:], in1=pf[:, 2 * NJ : 3 * NJ], op=ALU.add)
         r = math.sqrt(C2)
         sc1 = const.tile([P, NJ], F32)
         bi1 = const.tile([P, NJ], F32)
@@ -124,18 +112,6 @@ def tile_modelnew_kernel(
         sc2 = const.tile([P, NJ], F32)
         bi2 = const.tile([P, NJ], F32)
         bb = const.tile([P, NJ], F32)
-        nc.vector.tensor_scalar(out=sc1[:], in0=a_c[:], scalar1=r, scalar2=None, op0=ALU.mult)
-        nc.vector.tensor_scalar(out=bi1[:], in0=b_c[:], scalar1=1.5 * r, scalar2=None, op0=ALU.mult)
-        nc.vector.tensor_tensor(out=bb[:], in0=b_c[:], in1=b_c[:], op=ALU.mult)
-        nc.vector.tensor_scalar(
-            out=s_c[:], in0=bb[:], scalar1=0.75 * C2, scalar2=C1, op0=ALU.mult, op1=ALU.add
-        )
-        nc.vector.tensor_scalar(out=sc2[:], in0=a_c[:], scalar1=2.0, scalar2=None, op0=ALU.mult)
-        nc.vector.tensor_scalar(
-            out=bb[:], in0=bb[:], scalar1=2.0 * C2, scalar2=2.0 * C1, op0=ALU.mult, op1=ALU.add
-        )
-        nc.vector.tensor_tensor(out=bi2[:], in0=bb[:], in1=b_c[:], op=ALU.mult)
-
         nh_sgw = const.tile([P, 1], F32)
         mgb = const.tile([P, 1], F32)
 
@@ -166,7 +142,7 @@ def tile_modelnew_kernel(
 
         def pe_xt(g, b):
             if ok(g):
-                banks_of[(g, b)] = transposes(x_of[g][0], x_of[g][1], b)
+                banks_of[(g, b)] = transposes(x_of[g][0], x_of[g][1], b, "xt%d" % b)
 
         def evac(g, b, engine):
             if ok(g):
@@ -200,7 +176,7 @@ def tile_modelnew_kernel(
                     acc_of[(g, j)] = acc
 
         def z_on_vector(g, j):
-            return (g == 0 and j == 1) or (g == 1 and j in (1, 3))
+            return g in (0, 1) and j == 1
 
         def s_square_z(g, js):
             if ok(g):
@@ -295,24 +271,91 @@ def tile_modelnew_kernel(
                     accum_out=traw[:, tt : tt + 1],
                 )
 
-        for g in range(-2, NG + 2):
-            e0 = "v" if g in (0, 1) else "s"
+        w_grouped = work2.tile([P, GW * 4], BF16, tag="grouped", align_bytes=64)
+        copy_out(w_grouped, transposes(w_sb, 0, 0, "acc0"), 0, "s")
+        copy_out(w_grouped, transposes(w_sb, 0, 1, "acc1"), 1, "s")
+        pe_xt(0, 0)
+        evac(0, 0, "s")
+        pe_xt(0, 1)
+        evac(0, 1, "s")
+        nc.vector.quantize_mx(out=wq[:].bitcast(FP8X4), scales=ws[:], in_=w_grouped[:])
+        pT = psum.tile([P, P], BF16, tag="yT0", name="pT")
+        nc.tensor.transpose(pT[:], pv[:], ident_b[:])
+        nc.vector.tensor_copy(out=pf[:], in_=pT[:, 0 : 5 * NJ])
+        nc.vector.tensor_scalar(
+            out=a_c[:], in0=pf[:, 4 * NJ : 5 * NJ], scalar1=EPS, scalar2=None, op0=ALU.add
+        )
+        nc.gpsimd.tensor_tensor(out=a_c[:], in0=a_c[:], in1=mhalf[:], op=ALU.pow)
+        nc.vector.tensor_tensor(
+            out=b_c[:], in0=pf[:, 0:NJ], in1=pf[:, 3 * NJ : 4 * NJ], op=ALU.subtract
+        )
+        pe_xt(1, 0)
+        evac(1, 0, "s")
+        pe_xt(1, 1)
+        evac(1, 1, "s")
+        quant(0)
+        nc.vector.tensor_tensor(out=a_c[:], in0=a_c[:], in1=pf[:, NJ : 2 * NJ], op=ALU.mult)
+        nc.vector.tensor_tensor(out=b_c[:], in0=b_c[:], in1=a_c[:], op=ALU.mult)
+        nc.vector.tensor_tensor(out=b_c[:], in0=b_c[:], in1=pf[:, 2 * NJ : 3 * NJ], op=ALU.add)
+        nc.vector.tensor_scalar(out=sc1[:], in0=a_c[:], scalar1=r, scalar2=None, op0=ALU.mult)
+        nc.vector.tensor_scalar(out=bi1[:], in0=b_c[:], scalar1=1.5 * r, scalar2=None, op0=ALU.mult)
+        nc.vector.tensor_tensor(out=bb[:], in0=b_c[:], in1=b_c[:], op=ALU.mult)
+        nc.vector.tensor_scalar(
+            out=s_c[:], in0=bb[:], scalar1=0.75 * C2, scalar2=C1, op0=ALU.mult, op1=ALU.add
+        )
+        nc.vector.tensor_scalar(out=sc2[:], in0=a_c[:], scalar1=2.0, scalar2=None, op0=ALU.mult)
+        nc.vector.tensor_scalar(
+            out=bb[:], in0=bb[:], scalar1=2.0 * C2, scalar2=2.0 * C1, op0=ALU.mult, op1=ALU.add
+        )
+        nc.vector.tensor_tensor(out=bi2[:], in0=bb[:], in1=b_c[:], op=ALU.mult)
+        quant(1)
+        mx(0, (0, 1, 2, 3))
+        pe_xt(2, 0)
+        pe_xt(2, 1)
+
+        for g in (0, 1):
+            s_square_z(g, (0, 1))
+            s_sigmoid(g - 1, (2, 3))
+            g_mul(g - 1, (2, 3))
+            v_cubic(g, (0, 1))
+            evac(g + 2, 0, "v")
+            mx(g + 1, (0, 1))
+            if g == 1:
+                pe_xt(g + 3, 0)
+                pe_yt(g - 1, 0)
+                pe_yt(g - 1, 1)
+            s_square_z(g, (2, 3))
+            v_cubic(g, (2, 3))
+            evac(g + 2, 1, "v")
+            quant(g + 2)
+            mx(g + 1, (2, 3))
+            if g == 0:
+                pe_xt(g + 3, 0)
+            pe_xt(g + 3, 1)
+            s_sigmoid(g, (0, 1))
+            g_mul(g, (0, 1))
+        row_constants()
+
+        for g in range(2, NG + 2):
             e1 = "v" if g in V_COPIES else "s"
-            pe_xt(g + 2, 0)
+            if g > 2:
+                pe_xt(g + 2, 0)
             s_square_z(g, (0, 1))
             v_bn(g - 2, 0)
             v_dot(g - 2, 0)
             v_bn(g - 2, 1)
             v_dot(g - 2, 1)
-            evac(g + 2, 0, e0)
+            evac(g + 2, 0, "s")
             pe_yt(g - 2, 2)
             pe_yt(g - 2, 3)
-            quant(g + 1)
+            if g > 2:
+                quant(g + 1)
             s_sigmoid(g - 1, (2, 3))
             g_mul(g - 1, (2, 3))
             v_cubic(g, (0, 1))
             mx(g + 1, (0, 1))
-            pe_xt(g + 2, 1)
+            if g > 2:
+                pe_xt(g + 2, 1)
             s_square_z(g, (2, 3))
             v_bn(g - 2, 2)
             v_dot(g - 2, 2)
@@ -320,16 +363,11 @@ def tile_modelnew_kernel(
             v_dot(g - 2, 3)
             pe_yt(g - 1, 0)
             pe_yt(g - 1, 1)
-            if e1 == "s":
-                evac(g + 2, 1, "s")
             v_cubic(g, (2, 3))
             mx(g + 1, (2, 3))
             s_sigmoid(g, (0, 1))
             g_mul(g, (0, 1))
-            if e1 == "v":
-                evac(g + 2, 1, "v")
-            if g == 1:
-                row_constants()
+            evac(g + 2, 1, e1)
 
         warm = const.tile([P, 1], F32)
         nc.scalar.activation(out=warm[:], in_=eps1[:], func=ACT.Sqrt, bias=eps1[:, 0:1], scale=1.0)
@@ -337,21 +375,23 @@ def tile_modelnew_kernel(
         s = const.tile([P, NT], F32)
         d = const.tile([P, NT], F32)
         vs = const.tile([P, NT], F32)
-        nc.vector.tensor_tensor(out=s[:], in0=st[:, :, 1], in1=st[:, :, 4], op=ALU.add)
         nc.vector.tensor_tensor(out=d[:], in0=st[:, :, 1], in1=st[:, :, 4], op=ALU.subtract)
         nc.vector.tensor_tensor(out=vs[:], in0=st[:, :, 2], in1=st[:, :, 5], op=ALU.add)
-        nc.vector.tensor_tensor(out=d[:], in0=d[:], in1=d[:], op=ALU.mult)
         nc.vector.scalar_tensor_tensor(
-            out=vs[:], in0=d[:], scalar=float(OUT // 4), in1=vs[:], op0=ALU.mult, op1=ALU.add
+            out=d[:], in0=d[:], scalar=float(OUT // 4), in1=d[:], op0=ALU.mult, op1=ALU.mult
         )
+        nc.vector.tensor_tensor(out=vs[:], in0=vs[:], in1=d[:], op=ALU.add)
         nc.scalar.activation(
             out=vs[:], in_=vs[:], func=ACT.Sqrt, bias=eps2[:, 0:1], scale=float(OUT)
         )
-        nc.vector.reciprocal(out=vs[:], in_=vs[:])
+        nc.vector.tensor_tensor(out=s[:], in0=st[:, :, 1], in1=st[:, :, 4], op=ALU.add)
         nc.vector.scalar_tensor_tensor(
             out=s[:], in0=s[:], scalar=nh_sgw[:, 0:1], in1=traw[:], op0=ALU.mult, op1=ALU.add
         )
+        nc.vector.reciprocal(out=vs[:], in_=vs[:])
         nc.vector.tensor_tensor(out=s[:], in0=s[:], in1=vs[:], op=ALU.mult)
         res = const.tile([P, NT], F32)
-        nc.scalar.activation(out=res[:], in_=s[:], func=ACT.Relu, bias=mgb[:, 0:1], scale=1.0)
+        nc.vector.tensor_scalar(
+            out=res[:], in0=s[:], scalar1=mgb[:, 0:1], scalar2=0.0, op0=ALU.add, op1=ALU.max
+        )
         nc.sync.dma_start(out=out.rearrange("(p t) o -> p (t o)", t=NT), in_=res[:])

@@ -23,7 +23,8 @@ GW = GT * P
 NG = NT // GT
 CHUNKS = (4, 4) + (8,) * 15
 NJ = OUT // P
-V_COPIES = (7, 13, 19, 25)
+X_TWO_BANKS = 5
+LAST_GP = 28
 
 FLOPS = 2 * B * IN * OUT
 
@@ -38,6 +39,7 @@ def tile_modelnew_kernel(
         xin = ctx.enter_context(tc.tile_pool(name="xin", bufs=1))
         work2 = ctx.enter_context(tc.tile_pool(name="work2", bufs=2))
         work3 = ctx.enter_context(tc.tile_pool(name="work3", bufs=3))
+        work4 = ctx.enter_context(tc.tile_pool(name="work4", bufs=4))
         psum = ctx.enter_context(tc.psum_pool(name="psum", bufs=1))
 
         w_sb = const.tile([P, NJ * IN], BF16)
@@ -47,7 +49,7 @@ def tile_modelnew_kernel(
         )
         pv = const.tile([P, P], BF16)
         nc.gpsimd.memset(pv[:], 0.0)
-        for v, vec in enumerate((bias, bn_weight, bn_bias, bn_mean, bn_var)):
+        for v, vec in enumerate((bias, bn_weight, bn_bias, bn_mean, bn_var, gn_weight)):
             nc.scalar.dma_start(
                 out=pv[NJ * v : NJ * v + NJ, :], in_=vec.rearrange("(j p) -> j p", p=P)
             )
@@ -102,7 +104,7 @@ def tile_modelnew_kernel(
 
         wq = const.tile([P, OUT], U32, align_bytes=64)
         ws = const.tile([P, OUT], U8, align_bytes=64)
-        pf = const.tile([P, 5 * NJ], F32)
+        pf = const.tile([P, 6 * NJ], F32)
         a_c = const.tile([P, NJ], F32)
         b_c = const.tile([P, NJ], F32)
         r = math.sqrt(C2)
@@ -115,19 +117,10 @@ def tile_modelnew_kernel(
         nh_sgw = const.tile([P, 1], F32)
         mgb = const.tile([P, 1], F32)
 
-        def row_constants():
-            nc.vector.tensor_reduce(out=nh_sgw[:], in_=gwb[:], axis=AX.X, op=ALU.add)
-            nc.vector.tensor_scalar(
-                out=nh_sgw[:], in0=nh_sgw[:], scalar1=-0.5, scalar2=None, op0=ALU.mult
-            )
-            nc.vector.tensor_reduce(out=mgb[:], in_=gbb[:], axis=AX.X, op=ALU.add)
-            nc.vector.tensor_scalar(
-                out=mgb[:], in0=mgb[:], scalar1=1.0 / OUT, scalar2=None, op0=ALU.mult
-            )
-
         st = const.tile([P, NT, 6], F32)
         traw = const.tile([P, NT], F32)
         junk = const.tile([P, OUT], F32)
+        junk_s = const.tile([P, OUT], F32)
 
         banks_of = {}
         grouped_of = {}
@@ -142,7 +135,8 @@ def tile_modelnew_kernel(
 
         def pe_xt(g, b):
             if ok(g):
-                banks_of[(g, b)] = transposes(x_of[g][0], x_of[g][1], b, "xt%d" % b)
+                tag = "xt%d" % b if g < X_TWO_BANKS else "xt0"
+                banks_of[(g, b)] = transposes(x_of[g][0], x_of[g][1], b, tag)
 
         def evac(g, b, engine):
             if ok(g):
@@ -181,7 +175,7 @@ def tile_modelnew_kernel(
         def s_square_z(g, js):
             if ok(g):
                 if js[0] == 0:
-                    c_of[g] = work3.tile([P, NJ * GW], F32, tag="c", name="c")
+                    c_of[g] = work4.tile([P, NJ * GW], F32, tag="c", name="c")
                     z_of[g] = work3.tile([P, NJ * GW], F32, tag="z", name="z")
                 for j in js:
                     if not z_on_vector(g, j):
@@ -236,11 +230,51 @@ def tile_modelnew_kernel(
 
         def g_mul(g, js):
             if ok(g):
+                cols = slice(js[0] * GW, (js[-1] + 1) * GW)
+                nc.gpsimd.tensor_tensor(
+                    out=c_of[g][:, cols], in0=c_of[g][:, cols], in1=z_of[g][:, cols], op=ALU.mult
+                )
+
+        w_of = {}
+        w4_of = {}
+
+        def by_gpsimd(g):
+            return 0 <= g <= LAST_GP
+
+        def g_weigh(g, js):
+            if by_gpsimd(g):
+                if js[0] == 0:
+                    w_of[g] = work2.tile([P, NJ, P], F32, tag="w", name="w")
                 for j in js:
-                    cj = c_of[g][:, j * GW : (j + 1) * GW]
-                    nc.gpsimd.tensor_tensor(
-                        out=cj, in0=cj, in1=z_of[g][:, j * GW : (j + 1) * GW], op=ALU.mult
+                    nc.gpsimd.tensor_scalar(
+                        out=w_of[g][:, j, :],
+                        in0=c_of[g][:, j * GW + (GT - 1) * P : (j + 1) * GW],
+                        scalar1=pf[:, 5 * NJ + j : 5 * NJ + j + 1],
+                        scalar2=zero[:, 0:1],
+                        op0=ALU.mult,
+                        op1=ALU.add,
                     )
+
+        def pe_wt(g):
+            if by_gpsimd(g):
+                w4 = psum.tile([P, P], F32, tag="xt1", name="w4")
+                for j in range(NJ):
+                    nc.tensor.matmul(
+                        out=w4[:],
+                        lhsT=w_of[g][:, j, :],
+                        rhs=ident[:],
+                        is_transpose=True,
+                        start=(j == 0),
+                        stop=(j == NJ - 1),
+                    )
+                w4_of[g] = w4
+
+        def v_red(g):
+            if by_gpsimd(g):
+                tt = g * GT + GT - 1
+                nc.vector.tensor_reduce(
+                    out=traw[:, tt : tt + 1], in_=w4_of[g][:], axis=AX.X, op=ALU.add
+                )
 
         def pe_yt(g, t):
             if ok(g):
@@ -258,7 +292,7 @@ def tile_modelnew_kernel(
                 nc.vector.bn_stats(out=st[:, g * GT + t, :], in_=yT_of[(g, t)][:])
 
         def v_dot(g, t):
-            if ok(g):
+            if ok(g) and not (t == GT - 1 and by_gpsimd(g)):
                 yT = yT_of[(g, t)]
                 tt = g * GT + t
                 nc.vector.scalar_tensor_tensor(
@@ -281,7 +315,7 @@ def tile_modelnew_kernel(
         nc.vector.quantize_mx(out=wq[:].bitcast(FP8X4), scales=ws[:], in_=w_grouped[:])
         pT = psum.tile([P, P], BF16, tag="yT0", name="pT")
         nc.tensor.transpose(pT[:], pv[:], ident_b[:])
-        nc.vector.tensor_copy(out=pf[:], in_=pT[:, 0 : 5 * NJ])
+        nc.vector.tensor_copy(out=pf[:], in_=pT[:, 0 : 6 * NJ])
         nc.vector.tensor_scalar(
             out=a_c[:], in0=pf[:, 4 * NJ : 5 * NJ], scalar1=EPS, scalar2=None, op0=ALU.add
         )
@@ -334,10 +368,9 @@ def tile_modelnew_kernel(
             pe_xt(g + 3, 1)
             s_sigmoid(g, (0, 1))
             g_mul(g, (0, 1))
-        row_constants()
 
         for g in range(2, NG + 2):
-            e1 = "v" if g in V_COPIES else "s"
+            e0 = "v" if g % 2 == 1 else "s"
             if g > 2:
                 pe_xt(g + 2, 0)
             s_square_z(g, (0, 1))
@@ -345,13 +378,15 @@ def tile_modelnew_kernel(
             v_dot(g - 2, 0)
             v_bn(g - 2, 1)
             v_dot(g - 2, 1)
-            evac(g + 2, 0, "s")
+            evac(g + 2, 0, e0)
             pe_yt(g - 2, 2)
             pe_yt(g - 2, 3)
+            pe_wt(g - 3)
             if g > 2:
                 quant(g + 1)
             s_sigmoid(g - 1, (2, 3))
             g_mul(g - 1, (2, 3))
+            g_weigh(g - 2, (0, 1))
             v_cubic(g, (0, 1))
             mx(g + 1, (0, 1))
             if g > 2:
@@ -361,14 +396,22 @@ def tile_modelnew_kernel(
             v_dot(g - 2, 2)
             v_bn(g - 2, 3)
             v_dot(g - 2, 3)
+            v_red(g - 3)
             pe_yt(g - 1, 0)
             pe_yt(g - 1, 1)
             v_cubic(g, (2, 3))
             mx(g + 1, (2, 3))
             s_sigmoid(g, (0, 1))
             g_mul(g, (0, 1))
-            evac(g + 2, 1, e1)
+            g_weigh(g - 2, (2, 3))
+            evac(g + 2, 1, "s")
 
+        nc.scalar.activation(
+            out=junk_s[:], in_=gwb[:], func=ACT.Copy, scale=-0.5, accum_out=nh_sgw[:, 0:1]
+        )
+        nc.scalar.activation(
+            out=junk_s[:], in_=gbb[:], func=ACT.Copy, scale=1.0 / OUT, accum_out=mgb[:, 0:1]
+        )
         warm = const.tile([P, 1], F32)
         nc.scalar.activation(out=warm[:], in_=eps1[:], func=ACT.Sqrt, bias=eps1[:, 0:1], scale=1.0)
 

import math
from contextlib import ExitStack

import concourse.mybir as mybir
from concourse.masks import make_identity

F32 = mybir.dt.float32
BF16 = mybir.dt.bfloat16
U32 = mybir.dt.uint32
U8 = mybir.dt.uint8
FP8X4 = mybir.dt.float8_e4m3fn_x4
ACT = mybir.ActivationFunctionType
ALU = mybir.AluOpType
AX = mybir.AxisListType

P = 128
B, IN, OUT = 16384, 512, 512
EPS = 1e-5
C1, C2 = 0.797885, 0.035677
NT = B // P
GT = 4
GW = GT * P
NG = NT // GT
CHUNKS = (4, 4) + (8,) * 15
NJ = OUT // P
X_TWO_BANKS = 5
LAST_GP = 28

FLOPS = 2 * B * IN * OUT


def tile_modelnew_kernel(
    tc, x, weight, bias, bn_weight, bn_bias, bn_mean, bn_var, gn_weight, gn_bias, out
):
    nc = tc.nc
    with ExitStack() as ctx:
        ctx.enter_context(tc.manual_schedule())
        const = ctx.enter_context(tc.tile_pool(name="const", bufs=1))
        xin = ctx.enter_context(tc.tile_pool(name="xin", bufs=1))
        work2 = ctx.enter_context(tc.tile_pool(name="work2", bufs=2))
        work3 = ctx.enter_context(tc.tile_pool(name="work3", bufs=3))
        work4 = ctx.enter_context(tc.tile_pool(name="work4", bufs=4))
        psum = ctx.enter_context(tc.psum_pool(name="psum", bufs=1))

        w_sb = const.tile([P, NJ * IN], BF16)
        nc.sync.dma_start(
            out=w_sb[:].rearrange("p (j k) -> p j k", k=IN),
            in_=weight.rearrange("(j p) k -> p j k", p=P),
        )
        pv = const.tile([P, P], BF16)
        nc.gpsimd.memset(pv[:], 0.0)
        for v, vec in enumerate((bias, bn_weight, bn_bias, bn_mean, bn_var, gn_weight)):
            nc.scalar.dma_start(
                out=pv[NJ * v : NJ * v + NJ, :], in_=vec.rearrange("(j p) -> j p", p=P)
            )
        zero = const.tile([P, 1], F32)
        nc.vector.memset(zero[:], 0.0)
        mhalf = const.tile([P, NJ], F32)
        nc.vector.memset(mhalf[:], -0.5)
        eps1 = const.tile([P, 1], F32)
        nc.vector.memset(eps1[:], EPS)
        eps2 = const.tile([P, 1], F32)
        nc.vector.memset(eps2[:], EPS * OUT * OUT)
        warm0 = const.tile([P, 1], F32)
        nc.scalar.activation(out=warm0[:], in_=zero[:], func=ACT.Sigmoid, bias=zero[:, 0:1], scale=1.0)
        gwb = const.tile([P, OUT], BF16)
        gbb = const.tile([P, OUT], BF16)

        x_rows = x.rearrange("(p t) k -> p (t k)", t=NT)
        x_of = []
        t0 = 0
        for c, n_tiles in enumerate(CHUNKS):
            xc = xin.tile([P, n_tiles * IN], BF16, tag="x%d" % c, name="xc")
            nc.sync.dma_start(out=xc[:], in_=x_rows[:, t0 * IN : (t0 + n_tiles) * IN])
            for q in range(n_tiles // GT):
                x_of.append((xc, q * GT * IN))
            t0 += n_tiles
            if c == 2:
                nc.sync.dma_start(out=gwb[:], in_=gn_weight.partition_broadcast(P))
                nc.sync.dma_start(out=gbb[:], in_=gn_bias.partition_broadcast(P))

        ident = const.tile([P, P], F32)
        make_identity(nc, ident[:])
        ident_b = const.tile([P, P], BF16)
        make_identity(nc, ident_b[:])

        def transposes(src, col0, b, tag):
            words = src[:].bitcast(F32)
            xt = psum.tile([P, 2, 2, P], F32, tag=tag, name="xt_" + tag)
            for t2 in range(2):
                for u in range(2):
                    w0 = col0 // 2 + (2 * b + t2) * (IN // 2) + u * P
                    nc.tensor.transpose(xt[:, t2, u, :], words[:, w0 : w0 + P], ident[:])
            return xt

        def copy_out(grouped, xt, b, engine):
            gw32 = grouped[:].bitcast(F32)
            dst = gw32[:, b * 512 : (b + 1) * 512].rearrange("p (t r u) -> p t r u", t=2, u=2)
            srcv = xt[:].rearrange("p t u r -> p t r u")
            if engine == "s":
                nc.scalar.copy(out=dst, in_=srcv)
            else:
                nc.vector.tensor_copy(out=dst, in_=srcv)

        wq = const.tile([P, OUT], U32, align_bytes=64)
        ws = const.tile([P, OUT], U8, align_bytes=64)
        pf = const.tile([P, 6 * NJ], F32)
        a_c = const.tile([P, NJ], F32)
        b_c = const.tile([P, NJ], F32)
        r = math.sqrt(C2)
        sc1 = const.tile([P, NJ], F32)
        bi1 = const.tile([P, NJ], F32)
        s_c = const.tile([P, NJ], F32)
        sc2 = const.tile([P, NJ], F32)
        bi2 = const.tile([P, NJ], F32)
        bb = const.tile([P, NJ], F32)
        nh_sgw = const.tile([P, 1], F32)
        mgb = const.tile([P, 1], F32)

        st = const.tile([P, NT, 6], F32)
        traw = const.tile([P, NT], F32)
        junk = const.tile([P, OUT], F32)
        junk_s = const.tile([P, OUT], F32)

        banks_of = {}
        grouped_of = {}
        xq_of = {}
        acc_of = {}
        c_of = {}
        z_of = {}
        yT_of = {}

        def ok(g):
            return 0 <= g < NG

        def pe_xt(g, b):
            if ok(g):
                tag = "xt%d" % b if g < X_TWO_BANKS else "xt0"
                banks_of[(g, b)] = transposes(x_of[g][0], x_of[g][1], b, tag)

        def evac(g, b, engine):
            if ok(g):
                if b == 0:
                    grouped_of[g] = work2.tile(
                        [P, GW * 4], BF16, tag="grouped", name="grouped", align_bytes=64
                    )
                copy_out(grouped_of[g], banks_of[(g, b)], b, engine)

        def quant(g):
            if ok(g):
                xq = work2.tile([P, GW], U32, tag="xq", align_bytes=64)
                xs = work2.tile([P, GW], U8, tag="xs", align_bytes=64)
                nc.vector.quantize_mx(out=xq[:].bitcast(FP8X4), scales=xs[:], in_=grouped_of[g][:])
                xq_of[g] = (xq, xs)

        def mx(g, js):
            if ok(g):
                xq, xs = xq_of[g]
                for j in js:
                    acc = psum.tile([P, GW], F32, tag="acc%d" % j, name="acc%d" % j)
                    nc.tensor.matmul_mx(
                        out=acc[:],
                        lhsT=wq[:, j * P : (j + 1) * P].bitcast(FP8X4),
                        lhsT_scale=ws[:, j * P : (j + 1) * P],
                        rhs=xq[:].bitcast(FP8X4),
                        rhs_scale=xs[:],
                        start=True,
                        stop=True,
                    )
                    acc_of[(g, j)] = acc

        def z_on_vector(g, j):
            return g in (0, 1) and j == 1

        def s_square_z(g, js):
            if ok(g):
                if js[0] == 0:
                    c_of[g] = work4.tile([P, NJ * GW], F32, tag="c", name="c")
                    z_of[g] = work3.tile([P, NJ * GW], F32, tag="z", name="z")
                for j in js:
                    if not z_on_vector(g, j):
                        nc.scalar.activation(
                            out=z_of[g][:, j * GW : (j + 1) * GW],
                            in_=acc_of[(g, j)][:],
                            func=ACT.Identity,
                            bias=b_c[:, j : j + 1],
                            scale=a_c[:, j : j + 1],
                        )
                    nc.scalar.activation(
                        out=c_of[g][:, j * GW : (j + 1) * GW],
                        in_=acc_of[(g, j)][:],
                        func=ACT.Square,
                        bias=bi1[:, j : j + 1],
                        scale=sc1[:, j : j + 1],
                    )

        def v_cubic(g, js):
            if ok(g):
                for j in js:
                    cj = c_of[g][:, j * GW : (j + 1) * GW]
                    nc.vector.scalar_tensor_tensor(
                        out=cj,
                        in0=cj,
                        scalar=s_c[:, j : j + 1],
                        in1=acc_of[(g, j)][:],
                        op0=ALU.add,
                        op1=ALU.mult,
                    )
                    if z_on_vector(g, j):
                        nc.vector.tensor_scalar(
                            out=z_of[g][:, j * GW : (j + 1) * GW],
                            in0=acc_of[(g, j)][:],
                            scalar1=a_c[:, j : j + 1],
                            scalar2=b_c[:, j : j + 1],
                            op0=ALU.mult,
                            op1=ALU.add,
                        )

        def s_sigmoid(g, js):
            if ok(g):
                for j in js:
                    cj = c_of[g][:, j * GW : (j + 1) * GW]
                    nc.scalar.activation(
                        out=cj,
                        in_=cj,
                        func=ACT.Sigmoid,
                        bias=bi2[:, j : j + 1],
                        scale=sc2[:, j : j + 1],
                    )

        def g_mul(g, js):
            if ok(g):
                cols = slice(js[0] * GW, (js[-1] + 1) * GW)
                nc.gpsimd.tensor_tensor(
                    out=c_of[g][:, cols], in0=c_of[g][:, cols], in1=z_of[g][:, cols], op=ALU.mult
                )

        w_of = {}
        w4_of = {}

        def by_gpsimd(g):
            return 0 <= g <= LAST_GP

        def g_weigh(g, js):
            if by_gpsimd(g):
                if js[0] == 0:
                    w_of[g] = work2.tile([P, NJ, P], F32, tag="w", name="w")
                for j in js:
                    nc.gpsimd.tensor_scalar(
                        out=w_of[g][:, j, :],
                        in0=c_of[g][:, j * GW + (GT - 1) * P : (j + 1) * GW],
                        scalar1=pf[:, 5 * NJ + j : 5 * NJ + j + 1],
                        scalar2=zero[:, 0:1],
                        op0=ALU.mult,
                        op1=ALU.add,
                    )

        def pe_wt(g):
            if by_gpsimd(g):
                w4 = psum.tile([P, P], F32, tag="xt1", name="w4")
                for j in range(NJ):
                    nc.tensor.matmul(
                        out=w4[:],
                        lhsT=w_of[g][:, j, :],
                        rhs=ident[:],
                        is_transpose=True,
                        start=(j == 0),
                        stop=(j == NJ - 1),
                    )
                w4_of[g] = w4

        def v_red(g):
            if by_gpsimd(g):
                tt = g * GT + GT - 1
                nc.vector.tensor_reduce(
                    out=traw[:, tt : tt + 1], in_=w4_of[g][:], axis=AX.X, op=ALU.add
                )

        def pe_yt(g, t):
            if ok(g):
                yT = psum.tile([P, OUT], F32, tag="yT%d" % (t % 2), name="yT%d" % (t % 2))
                for j in range(NJ):
                    nc.tensor.transpose(
                        yT[:, j * P : (j + 1) * P],
                        c_of[g][:, j * GW + t * P : j * GW + (t + 1) * P],
                        ident[:],
                    )
                yT_of[(g, t)] = yT

        def v_bn(g, t):
            if ok(g):
                nc.vector.bn_stats(out=st[:, g * GT + t, :], in_=yT_of[(g, t)][:])

        def v_dot(g, t):
            if ok(g) and not (t == GT - 1 and by_gpsimd(g)):
                yT = yT_of[(g, t)]
                tt = g * GT + t
                nc.vector.scalar_tensor_tensor(
                    out=junk[:],
                    in0=yT[:],
                    scalar=1.0,
                    in1=gwb[:],
                    op0=ALU.mult,
                    op1=ALU.mult,
                    accum_out=traw[:, tt : tt + 1],
                )

        w_grouped = work2.tile([P, GW * 4], BF16, tag="grouped", align_bytes=64)
        copy_out(w_grouped, transposes(w_sb, 0, 0, "acc0"), 0, "s")
        copy_out(w_grouped, transposes(w_sb, 0, 1, "acc1"), 1, "s")
        pe_xt(0, 0)
        evac(0, 0, "s")
        pe_xt(0, 1)
        evac(0, 1, "s")
        nc.vector.quantize_mx(out=wq[:].bitcast(FP8X4), scales=ws[:], in_=w_grouped[:])
        pT = psum.tile([P, P], BF16, tag="yT0", name="pT")
        nc.tensor.transpose(pT[:], pv[:], ident_b[:])
        nc.vector.tensor_copy(out=pf[:], in_=pT[:, 0 : 6 * NJ])
        nc.vector.tensor_scalar(
            out=a_c[:], in0=pf[:, 4 * NJ : 5 * NJ], scalar1=EPS, scalar2=None, op0=ALU.add
        )
        nc.gpsimd.tensor_tensor(out=a_c[:], in0=a_c[:], in1=mhalf[:], op=ALU.pow)
        nc.vector.tensor_tensor(
            out=b_c[:], in0=pf[:, 0:NJ], in1=pf[:, 3 * NJ : 4 * NJ], op=ALU.subtract
        )
        pe_xt(1, 0)
        evac(1, 0, "s")
        pe_xt(1, 1)
        evac(1, 1, "s")
        quant(0)
        nc.vector.tensor_tensor(out=a_c[:], in0=a_c[:], in1=pf[:, NJ : 2 * NJ], op=ALU.mult)
        nc.vector.tensor_tensor(out=b_c[:], in0=b_c[:], in1=a_c[:], op=ALU.mult)
        nc.vector.tensor_tensor(out=b_c[:], in0=b_c[:], in1=pf[:, 2 * NJ : 3 * NJ], op=ALU.add)
        nc.vector.tensor_scalar(out=sc1[:], in0=a_c[:], scalar1=r, scalar2=None, op0=ALU.mult)
        nc.vector.tensor_scalar(out=bi1[:], in0=b_c[:], scalar1=1.5 * r, scalar2=None, op0=ALU.mult)
        nc.vector.tensor_tensor(out=bb[:], in0=b_c[:], in1=b_c[:], op=ALU.mult)
        nc.vector.tensor_scalar(
            out=s_c[:], in0=bb[:], scalar1=0.75 * C2, scalar2=C1, op0=ALU.mult, op1=ALU.add
        )
        nc.vector.tensor_scalar(out=sc2[:], in0=a_c[:], scalar1=2.0, scalar2=None, op0=ALU.mult)
        nc.vector.tensor_scalar(
            out=bb[:], in0=bb[:], scalar1=2.0 * C2, scalar2=2.0 * C1, op0=ALU.mult, op1=ALU.add
        )
        nc.vector.tensor_tensor(out=bi2[:], in0=bb[:], in1=b_c[:], op=ALU.mult)
        quant(1)
        mx(0, (0, 1, 2, 3))
        pe_xt(2, 0)
        pe_xt(2, 1)

        for g in (0, 1):
            s_square_z(g, (0, 1))
            s_sigmoid(g - 1, (2, 3))
            g_mul(g - 1, (2, 3))
            v_cubic(g, (0, 1))
            evac(g + 2, 0, "v")
            mx(g + 1, (0, 1))
            if g == 1:
                pe_xt(g + 3, 0)
                pe_yt(g - 1, 0)
                pe_yt(g - 1, 1)
            s_square_z(g, (2, 3))
            v_cubic(g, (2, 3))
            evac(g + 2, 1, "v")
            quant(g + 2)
            mx(g + 1, (2, 3))
            if g == 0:
                pe_xt(g + 3, 0)
            pe_xt(g + 3, 1)
            s_sigmoid(g, (0, 1))
            g_mul(g, (0, 1))

        for g in range(2, NG + 2):
            e0 = "v" if g % 2 == 1 else "s"
            if g > 2:
                pe_xt(g + 2, 0)
            s_square_z(g, (0, 1))
            v_bn(g - 2, 0)
            v_dot(g - 2, 0)
            v_bn(g - 2, 1)
            v_dot(g - 2, 1)
            evac(g + 2, 0, e0)
            pe_yt(g - 2, 2)
            pe_yt(g - 2, 3)
            pe_wt(g - 3)
            if g > 2:
                quant(g + 1)
            s_sigmoid(g - 1, (2, 3))
            g_mul(g - 1, (2, 3))
            g_weigh(g - 2, (0, 1))
            v_cubic(g, (0, 1))
            mx(g + 1, (0, 1))
            if g > 2:
                pe_xt(g + 2, 1)
            s_square_z(g, (2, 3))
            v_bn(g - 2, 2)
            v_dot(g - 2, 2)
            v_bn(g - 2, 3)
            v_dot(g - 2, 3)
            v_red(g - 3)
            pe_yt(g - 1, 0)
            pe_yt(g - 1, 1)
            v_cubic(g, (2, 3))
            mx(g + 1, (2, 3))
            s_sigmoid(g, (0, 1))
            g_mul(g, (0, 1))
            g_weigh(g - 2, (2, 3))
            evac(g + 2, 1, "s")

        nc.scalar.activation(
            out=junk_s[:], in_=gwb[:], func=ACT.Copy, scale=-0.5, accum_out=nh_sgw[:, 0:1]
        )
        nc.scalar.activation(
            out=junk_s[:], in_=gbb[:], func=ACT.Copy, scale=1.0 / OUT, accum_out=mgb[:, 0:1]
        )
        warm = const.tile([P, 1], F32)
        nc.scalar.activation(out=warm[:], in_=eps1[:], func=ACT.Sqrt, bias=eps1[:, 0:1], scale=1.0)

        s = const.tile([P, NT], F32)
        d = const.tile([P, NT], F32)
        vs = const.tile([P, NT], F32)
        nc.vector.tensor_tensor(out=d[:], in0=st[:, :, 1], in1=st[:, :, 4], op=ALU.subtract)
        nc.vector.tensor_tensor(out=vs[:], in0=st[:, :, 2], in1=st[:, :, 5], op=ALU.add)
        nc.vector.scalar_tensor_tensor(
            out=d[:], in0=d[:], scalar=float(OUT // 4), in1=d[:], op0=ALU.mult, op1=ALU.mult
        )
        nc.vector.tensor_tensor(out=vs[:], in0=vs[:], in1=d[:], op=ALU.add)
        nc.scalar.activation(
            out=vs[:], in_=vs[:], func=ACT.Sqrt, bias=eps2[:, 0:1], scale=float(OUT)
        )
        nc.vector.tensor_tensor(out=s[:], in0=st[:, :, 1], in1=st[:, :, 4], op=ALU.add)
        nc.vector.scalar_tensor_tensor(
            out=s[:], in0=s[:], scalar=nh_sgw[:, 0:1], in1=traw[:], op0=ALU.mult, op1=ALU.add
        )
        nc.vector.reciprocal(out=vs[:], in_=vs[:])
        nc.vector.tensor_tensor(out=s[:], in0=s[:], in1=vs[:], op=ALU.mult)
        res = const.tile([P, NT], F32)
        nc.vector.tensor_scalar(
            out=res[:], in0=s[:], scalar1=mgb[:, 0:1], scalar2=0.0, op0=ALU.add, op1=ALU.max
        )
        nc.sync.dma_start(out=out.rearrange("(p t) o -> p (t o)", t=NT), in_=res[:])
